import numpy as np
import ml_dtypes


def mxq(x, axis, fmt="e4m3"):
    dtype, down = {"e4m3": (ml_dtypes.float8_e4m3fn, 7), "e5m2": (ml_dtypes.float8_e5m2, 14)}[fmt]
    v = np.moveaxis(np.asarray(x, np.float32).astype(ml_dtypes.bfloat16).astype(np.float64), axis, -1)
    blocks = v.reshape(v.shape[:-1] + (-1, 32))
    amax = np.abs(blocks).max(-1, keepdims=True)
    byte = np.maximum(np.where(amax > 0, np.frexp(amax)[1] - 1 + 127, 0) - down, 1)
    scale = np.exp2(byte - 127.0)
    codes = (blocks / scale).astype(np.float32).astype(dtype).astype(np.float64)
    return np.moveaxis((codes * scale).reshape(v.shape), -1, axis)


WIDE = False


def mx_kscale(k):
    if not WIDE:
        return np.ones(k)
    levels = np.array([10, -10, 5, -5, 0])
    a = np.random.permutation(np.resize(levels, k // 512 * 4)).reshape(k // 512, 4)
    idx = np.arange(k)
    return np.exp2(a[idx // 512, idx % 128 // 32])


BF16 = ml_dtypes.bfloat16


def bf(x):
    return np.asarray(x, np.float32).astype(BF16)


def f64(x):
    return np.asarray(x).astype(np.float64)


N, BI, BJ, C = 512, 256, 1024, 16
EPS = 1e-5


def layernorm(v, w, b):
    mu = v.mean(-1, keepdims=True)
    var = np.square(v - mu).mean(-1, keepdims=True)
    return (v - mu) * (1.0 / np.sqrt(var + EPS)) * w + b


def setup_inputs():
    s = mx_kscale(N)[None, :, None]
    return {"a_proj": bf(np.random.standard_normal((BI, N, C)) * 0.5 * s),
            "b_proj": bf(np.random.standard_normal((BJ, N, C)) * 0.5 / s),
            "ln2_w": bf(1.0 + 0.1 * np.random.standard_normal(C)),
            "ln2_b": bf(0.1 * np.random.standard_normal(C))}


def reference(a_proj, b_proj, ln2_w, ln2_b):
    at = np.ascontiguousarray(f64(a_proj).transpose(2, 0, 1))
    bt = np.ascontiguousarray(f64(b_proj).transpose(2, 1, 0))
    tri = mxq(at, 2, "e4m3") @ mxq(bt, 1, "e4m3")
    return layernorm(tri.transpose(1, 2, 0), f64(ln2_w), f64(ln2_b))

@@ -1,0 +1,183 @@
+from contextlib import ExitStack
+
+import concourse.mybir as mybir
+from concourse.masks import make_identity
+
+F32 = mybir.dt.float32
+BF16 = mybir.dt.bfloat16
+U32 = mybir.dt.uint32
+U8 = mybir.dt.uint8
+FP8X4 = mybir.dt.float8_e4m3fn_x4
+ALU = mybir.AluOpType
+ACT = mybir.ActivationFunctionType
+
+P = 128
+K = 512
+C = 16
+BI = 256
+BJ = 1024
+PACK = 4
+CP = C // 2
+J = 256
+EPS = 1e-5
+FLOPS = 2 * C * BI * BJ * K
+
+
+def tile_trianglemultiplication_pa_t_kernel(tc, a_proj, b_proj, ln2_w, ln2_b, out):
+    nc = tc.nc
+    with ExitStack() as ctx:
+        const = ctx.enter_context(tc.tile_pool(name="const", bufs=1))
+        natp = ctx.enter_context(tc.tile_pool(name="natp", bufs=2))
+        grp = ctx.enter_context(tc.tile_pool(name="grp", bufs=2))
+        bqp = ctx.enter_context(tc.tile_pool(name="bqp", bufs=2))
+        tp = ctx.enter_context(tc.tile_pool(name="tp", bufs=2))
+        sqp = ctx.enter_context(tc.tile_pool(name="sqp", bufs=1))
+        op = ctx.enter_context(tc.tile_pool(name="op", bufs=2))
+        small = ctx.enter_context(tc.tile_pool(name="small", bufs=2))
+        ps_tr = ctx.enter_context(tc.psum_pool(name="ps_tr", bufs=3))
+        ps_x = ctx.enter_context(tc.psum_pool(name="ps_x", bufs=2))
+        ps_sum = ctx.enter_context(tc.psum_pool(name="ps_sum", bufs=1))
+        ps_q = ctx.enter_context(tc.psum_pool(name="ps_q", bufs=1))
+        ps_r = ctx.enter_context(tc.psum_pool(name="ps_r", bufs=1))
+
+        ident = const.tile([P, P], F32, name="ident")
+        make_identity(nc, ident[:])
+        w_bf = const.tile([P, C], BF16, name="w_bf")
+        b_bf = const.tile([P, C], BF16, name="b_bf")
+        nc.scalar.dma_start(out=w_bf[:], in_=ln2_w.partition_broadcast(P))
+        nc.scalar.dma_start(out=b_bf[:], in_=ln2_b.partition_broadcast(P))
+        w_f = const.tile([P, C], F32, name="w_f")
+        b_f = const.tile([P, C], F32, name="b_f")
+        nc.vector.tensor_copy(out=w_f[:], in_=w_bf[:])
+        nc.vector.tensor_copy(out=b_f[:], in_=b_bf[:])
+        eps = const.tile([P, 1], F32, name="eps")
+        nc.vector.memset(eps[:], EPS)
+
+        a_codes = const.tile([P, BI // P, C, P], U32, name="a_codes", align_bytes=64)
+        a_scales = const.tile([P, BI // P, C, P], U8, name="a_scales", align_bytes=64)
+
+        def prep(rows, codes_of, scales_of, vector_share):
+            nat = natp.tile([P, K * C], BF16, name="nat")
+            nc.sync.dma_start(out=nat[:], in_=rows.rearrange("r k c -> r (k c)"))
+            words = nat[:].bitcast(F32).rearrange("p (q t w) -> p q t w", t=PACK, w=CP)
+            grouped = grp.tile([P, C, P, PACK], BF16, name="grouped", align_bytes=64)
+            for w in range(CP):
+                bank = ps_tr.tile([P, PACK * P], F32, name="bank")
+                for t in range(PACK):
+                    nc.tensor.transpose(bank[:, t * P:(t + 1) * P], words[:, :, t, w], ident[:])
+                src = bank[:].bitcast(BF16).rearrange("p (t r e) -> p e r t", t=PACK, e=2)
+                dst = grouped[:, 2 * w:2 * w + 2, :, :]
+                if w < vector_share:
+                    nc.vector.tensor_copy(out=dst, in_=src)
+                else:
+                    nc.scalar.copy(out=dst, in_=src)
+            for c in range(C):
+                nc.vector.quantize_mx(
+                    out=codes_of(c).bitcast(FP8X4),
+                    scales=scales_of(c),
+                    in_=grouped[:, c, :, :].rearrange("p r t -> p (r t)"),
+                )
+
+        def prep_a(it):
+            prep(
+                a_proj[it * P:(it + 1) * P, :, :],
+                lambda c: a_codes[:, it, c, :],
+                lambda c: a_scales[:, it, c, :],
+                4,
+            )
+
+        def prep_b(codes, scales, jp, h, vector_share):
+            r0 = jp * J + h * P
+            prep(
+                b_proj[r0:r0 + P, :, :],
+                lambda c: codes[:, c, h * P:(h + 1) * P],
+                lambda c: scales[:, c, h * P:(h + 1) * P],
+                vector_share,
+            )
+
+        def new_b():
+            codes = bqp.tile([P, C, J], U32, name="b_codes", align_bytes=64)
+            scales = bqp.tile([P, C, J], U8, name="b_scales", align_bytes=64)
+            return codes, scales
+
+        def mx(dst, it, codes, scales, c, start, stop):
+            nc.tensor.matmul_mx(
+                out=dst,
+                lhsT=a_codes[:, it, c, :].bitcast(FP8X4),
+                lhsT_scale=a_scales[:, it, c, :],
+                rhs=codes[:, c, :].bitcast(FP8X4),
+                rhs_scale=scales[:, c, :],
+                start=start,
+                stop=stop,
+            )
+
+        def unit(it, jp, codes, scales):
+            acc = ps_sum.tile([P, J], F32, name="acc")
+            for c in range(C):
+                mx(acc[:], it, codes, scales, c, c == 0, c == C - 1)
+            mu = small.tile([P, J], F32, name="mu")
+            nc.scalar.activation(out=mu[:], in_=acc[:], func=ACT.Copy, scale=1.0 / C)
+            t = tp.tile([P, C, J], F32, name="t")
+            for g in range(C // 2):
+                xb = ps_x.tile([P, 2, J], F32, name="xb")
+                for e in range(2):
+                    mx(xb[:, e, :], it, codes, scales, 2 * g + e, True, True)
+                nc.vector.tensor_tensor(
+                    out=t[:, 2 * g:2 * g + 2, :],
+                    in0=xb[:],
+                    in1=mu[:].unsqueeze(1).to_broadcast([P, 2, J]),
+                    op=ALU.subtract,
+                )
+            sq = sqp.tile([P, C, J], F32, name="sq")
+            for g in range(4):
+                nc.scalar.activation(out=sq[:, 4 * g:4 * g + 4, :], in_=t[:, 4 * g:4 * g + 4, :], func=ACT.Square)
+            q_t = ps_q.tile([P, J], F32, name="q_t")
+            for jb in range(J // P):
+                cols = slice(jb * P, (jb + 1) * P)
+                for c in range(C):
+                    nc.tensor.matmul(
+                        out=q_t[:, cols], lhsT=sq[:, c, cols], rhs=ident[:],
+                        is_transpose=True, start=(c == 0), stop=(c == C - 1),
+                    )
+            sig_t = small.tile([P, J], F32, name="sig_t")
+            nc.scalar.activation(out=sig_t[:], in_=q_t[:], func=ACT.Sqrt, scale=1.0 / C, bias=eps[:])
+            r_t = small.tile([P, J], F32, name="r_t")
+            nc.vector.reciprocal(out=r_t[:], in_=sig_t[:])
+            r = ps_r.tile([P, J], F32, name="r")
+            for jb in range(J // P):
+                cols = slice(jb * P, (jb + 1) * P)
+                nc.tensor.transpose(r[:, cols], r_t[:, cols], ident[:])
+            for c in range(C):
+                nc.vector.scalar_tensor_tensor(
+                    out=t[:, c, :], in0=t[:, c, :], scalar=w_f[:, c:c + 1], in1=r[:],
+                    op0=ALU.mult, op1=ALU.mult,
+                )
+            o = op.tile([P, J, C], F32, name="o")
+            for g in range(4):
+                nc.vector.tensor_tensor(
+                    out=o[:, :, 4 * g:4 * g + 4],
+                    in0=t[:, 4 * g:4 * g + 4, :].rearrange("p c j -> p j c"),
+                    in1=b_f[:, 4 * g:4 * g + 4].unsqueeze(1).to_broadcast([P, J, 4]),
+                    op=ALU.add,
+                )
+            nc.sync.dma_start(
+                out=out[it * P:(it + 1) * P, jp * J:(jp + 1) * J, :].rearrange("i j c -> i (j c)"),
+                in_=o[:].rearrange("p j c -> p (j c)"),
+            )
+
+        prep_a(0)
+        cur = new_b()
+        prep_b(cur[0], cur[1], 0, 0, 4)
+        prep_b(cur[0], cur[1], 0, 1, 4)
+        prep_a(1)
+        for jp in range(BJ // J):
+            nxt = None
+            if jp + 1 < BJ // J:
+                nxt = new_b()
+            unit(0, jp, cur[0], cur[1])
+            if nxt is not None:
+                prep_b(nxt[0], nxt[1], jp + 1, 0, 0)
+            unit(1, jp, cur[0], cur[1])
+            if nxt is not None:
+                prep_b(nxt[0], nxt[1], jp + 1, 1, 0)
+            cur = nxt

@@ -22,162 +22,316 @@ J = 256
 EPS = 1e-5
 FLOPS = 2 * C * BI * BJ * K
 
+NU = (BI // P) * (BJ // J)
+RING = 4
+XRING = 2
+XB = C // 2
+TILES = [("a", 0), ("b", 0), ("b", 1), ("a", 1)] + [("b", n) for n in range(2, BJ // P)]
+WARM = 24
+WARM_V = 2
+WARM_OF = 4
+S_A = [1,2,2,1,4,6,3,1,3]
+S_B = [1,5,2,1,3,2,0,4,2]
+S_C = [0,1,4,1,3,5,3,3,2]
+S_D = [3,3,0,3,0,0,4,2,0]
+V_X = [3,4,1,1,0,0,3,0,1]
+S_E = [0,2,0,1,0,1,3,1,1]
+
 
 def tile_trianglemultiplication_pa_t_kernel(tc, a_proj, b_proj, ln2_w, ln2_b, out):
     nc = tc.nc
     with ExitStack() as ctx:
         const = ctx.enter_context(tc.tile_pool(name="const", bufs=1))
-        natp = ctx.enter_context(tc.tile_pool(name="natp", bufs=2))
+        natp = ctx.enter_context(tc.tile_pool(name="natp", bufs=3))
         grp = ctx.enter_context(tc.tile_pool(name="grp", bufs=2))
         bqp = ctx.enter_context(tc.tile_pool(name="bqp", bufs=2))
-        tp = ctx.enter_context(tc.tile_pool(name="tp", bufs=2))
         sqp = ctx.enter_context(tc.tile_pool(name="sqp", bufs=1))
         op = ctx.enter_context(tc.tile_pool(name="op", bufs=2))
         small = ctx.enter_context(tc.tile_pool(name="small", bufs=2))
-        ps_tr = ctx.enter_context(tc.psum_pool(name="ps_tr", bufs=3))
-        ps_x = ctx.enter_context(tc.psum_pool(name="ps_x", bufs=2))
-        ps_sum = ctx.enter_context(tc.psum_pool(name="ps_sum", bufs=1))
-        ps_q = ctx.enter_context(tc.psum_pool(name="ps_q", bufs=1))
+        ps_tr = ctx.enter_context(tc.psum_pool(name="ps_tr", bufs=RING))
+        ps_x = ctx.enter_context(tc.psum_pool(name="ps_x", bufs=XRING))
+        ps_stat = ctx.enter_context(tc.psum_pool(name="ps_stat", bufs=1))
         ps_r = ctx.enter_context(tc.psum_pool(name="ps_r", bufs=1))
+        ctx.enter_context(tc.manual_schedule())
 
         ident = const.tile([P, P], F32, name="ident")
         make_identity(nc, ident[:])
         w_bf = const.tile([P, C], BF16, name="w_bf")
         b_bf = const.tile([P, C], BF16, name="b_bf")
-        nc.scalar.dma_start(out=w_bf[:], in_=ln2_w.partition_broadcast(P))
-        nc.scalar.dma_start(out=b_bf[:], in_=ln2_b.partition_broadcast(P))
         w_f = const.tile([P, C], F32, name="w_f")
         b_f = const.tile([P, C], F32, name="b_f")
-        nc.vector.tensor_copy(out=w_f[:], in_=w_bf[:])
-        nc.vector.tensor_copy(out=b_f[:], in_=b_bf[:])
         eps = const.tile([P, 1], F32, name="eps")
         nc.vector.memset(eps[:], EPS)
-
         a_codes = const.tile([P, BI // P, C, P], U32, name="a_codes", align_bytes=64)
         a_scales = const.tile([P, BI // P, C, P], U8, name="a_scales", align_bytes=64)
+        t_fixed = [const.tile([P, C, J], F32, name="t0"), const.tile([P, C, J], F32, name="t1")]
 
-        def prep(rows, codes_of, scales_of, vector_share):
-            nat = natp.tile([P, K * C], BF16, name="nat")
-            nc.sync.dma_start(out=nat[:], in_=rows.rearrange("r k c -> r (k c)"))
-            words = nat[:].bitcast(F32).rearrange("p (q t w) -> p q t w", t=PACK, w=CP)
-            grouped = grp.tile([P, C, P, PACK], BF16, name="grouped", align_bytes=64)
-            for w in range(CP):
-                bank = ps_tr.tile([P, PACK * P], F32, name="bank")
-                for t in range(PACK):
-                    nc.tensor.transpose(bank[:, t * P:(t + 1) * P], words[:, :, t, w], ident[:])
-                src = bank[:].bitcast(BF16).rearrange("p (t r e) -> p e r t", t=PACK, e=2)
-                dst = grouped[:, 2 * w:2 * w + 2, :, :]
-                if w < vector_share:
-                    nc.vector.tensor_copy(out=dst, in_=src)
-                else:
-                    nc.scalar.copy(out=dst, in_=src)
-            for c in range(C):
-                nc.vector.quantize_mx(
-                    out=codes_of(c).bitcast(FP8X4),
-                    scales=scales_of(c),
-                    in_=grouped[:, c, :, :].rearrange("p r t -> p (r t)"),
+        st = {"loaded": 0, "filled": 0, "exited": 0, "quantised": 0, "mx_done": 0}
+        nat = {}
+        grouped = {}
+        banks = {}
+        pair = {}
+        un = [dict() for u in range(NU)]
+
+        def load(n):
+            kind, idx = TILES[n]
+            src = a_proj if kind == "a" else b_proj
+            nat[n] = natp.tile([P, K * C], BF16, name="nat")
+            nc.sync.dma_start(out=nat[n][:], in_=src[idx * P:(idx + 1) * P, :, :].rearrange("r k c -> r (k c)"))
+            st["loaded"] = n + 1
+
+        def fill():
+            k = st["filled"]
+            n, w = k // CP, k % CP
+            words = nat[n][:].bitcast(F32).rearrange("p (q t w) -> p q t w", t=PACK, w=CP)
+            if k < WARM and k % 3 == 2:
+                banks[k] = ps_x.tile([P, PACK * P], F32, name="xb")
+            else:
+                banks[k] = ps_tr.tile([P, PACK * P], F32, name="bank")
+            for t in range(PACK):
+                nc.tensor.transpose(banks[k][:, t * P:(t + 1) * P], words[:, :, t, w], ident[:])
+            st["filled"] = k + 1
+            if w == CP - 1 and st["loaded"] < len(TILES):
+                load(st["loaded"])
+
+        def top_up():
+            ring = RING + XRING if st["filled"] < WARM else RING
+            while st["filled"] < min(st["exited"] + ring, CP * len(TILES)):
+                fill()
+
+        def leave(on_vector):
+            k = st["exited"]
+            if k >= CP * len(TILES):
+                return
+            if k >= st["filled"]:
+                top_up()
+            n, w = k // CP, k % CP
+            if w == 0:
+                grouped[n] = grp.tile([P, C, P, PACK], BF16, name="grouped", align_bytes=64)
+            src = banks[k][:].bitcast(BF16).rearrange("p (t r e) -> p e r t", t=PACK, e=2)
+            dst = grouped[n][:, 2 * w:2 * w + 2, :, :]
+            if on_vector:
+                nc.vector.tensor_copy(out=dst, in_=src)
+            else:
+                nc.scalar.copy(out=dst, in_=src)
+            st["exited"] = k + 1
+
+        def quantise(n):
+            kind, idx = TILES[n]
+            if kind == "b" and idx % 2 == 0:
+                pair[idx // 2] = (
+                    bqp.tile([P, C, J], U32, name="b_codes", align_bytes=64),
+                    bqp.tile([P, C, J], U8, name="b_scales", align_bytes=64),
                 )
+            for c in range(C):
+                if kind == "a":
+                    codes, scales = a_codes[:, idx, c, :], a_scales[:, idx, c, :]
+                else:
+                    h = idx % 2
+                    codes = pair[idx // 2][0][:, c, h * P:(h + 1) * P]
+                    scales = pair[idx // 2][1][:, c, h * P:(h + 1) * P]
+                nc.vector.quantize_mx(
+                    out=codes.bitcast(FP8X4), scales=scales,
+                    in_=grouped[n][:, c, :, :].rearrange("p r t -> p (r t)"),
+                )
+            st["quantised"] = n + 1
 
-        def prep_a(it):
-            prep(
-                a_proj[it * P:(it + 1) * P, :, :],
-                lambda c: a_codes[:, it, c, :],
-                lambda c: a_scales[:, it, c, :],
-                4,
-            )
+        def may_quantise(n):
+            kind, idx = TILES[n]
+            if st["exited"] < CP * (n + 1):
+                return False
+            return kind == "a" or idx // 2 < 2 or st["mx_done"] >= 2 * (idx // 2 - 2) + 2
 
-        def prep_b(codes, scales, jp, h, vector_share):
-            r0 = jp * J + h * P
-            prep(
-                b_proj[r0:r0 + P, :, :],
-                lambda c: codes[:, c, h * P:(h + 1) * P],
-                lambda c: scales[:, c, h * P:(h + 1) * P],
-                vector_share,
-            )
+        def quantise_ready():
+            while st["quantised"] < len(TILES) and may_quantise(st["quantised"]):
+                quantise(st["quantised"])
 
-        def new_b():
-            codes = bqp.tile([P, C, J], U32, name="b_codes", align_bytes=64)
-            scales = bqp.tile([P, C, J], U8, name="b_scales", align_bytes=64)
-            return codes, scales
+        def need(u):
+            last = TILES.index(("b", 2 * (u // 2) + 1))
+            last = max(last, TILES.index(("a", u % 2)))
+            while st["exited"] < CP * (last + 1):
+                leave(st["exited"] % 2 == 0)
+                top_up()
+            quantise_ready()
+            assert st["quantised"] > last
 
-        def mx(dst, it, codes, scales, c, start, stop):
+        def mx(dst, u, c, start, stop):
+            codes, scales = pair[u // 2]
             nc.tensor.matmul_mx(
                 out=dst,
-                lhsT=a_codes[:, it, c, :].bitcast(FP8X4),
-                lhsT_scale=a_scales[:, it, c, :],
-                rhs=codes[:, c, :].bitcast(FP8X4),
-                rhs_scale=scales[:, c, :],
-                start=start,
-                stop=stop,
+                lhsT=a_codes[:, u % 2, c, :].bitcast(FP8X4), lhsT_scale=a_scales[:, u % 2, c, :],
+                rhs=codes[:, c, :].bitcast(FP8X4), rhs_scale=scales[:, c, :],
+                start=start, stop=stop,
             )
 
-        def unit(it, jp, codes, scales):
-            acc = ps_sum.tile([P, J], F32, name="acc")
-            for c in range(C):
-                mx(acc[:], it, codes, scales, c, c == 0, c == C - 1)
-            mu = small.tile([P, J], F32, name="mu")
-            nc.scalar.activation(out=mu[:], in_=acc[:], func=ACT.Copy, scale=1.0 / C)
-            t = tp.tile([P, C, J], F32, name="t")
-            for g in range(C // 2):
-                xb = ps_x.tile([P, 2, J], F32, name="xb")
-                for e in range(2):
-                    mx(xb[:, e, :], it, codes, scales, 2 * g + e, True, True)
-                nc.vector.tensor_tensor(
-                    out=t[:, 2 * g:2 * g + 2, :],
-                    in0=xb[:],
-                    in1=mu[:].unsqueeze(1).to_broadcast([P, 2, J]),
-                    op=ALU.subtract,
+        def total(u, cs):
+            if cs[0] == 0:
+                un[u]["acc"] = ps_stat.tile([P, J], F32, name="stat")
+            for c in cs:
+                mx(un[u]["acc"][:], u, c, c == 0, c == C - 1)
+
+        def mean(u):
+            un[u]["mu"] = small.tile([P, J], F32, name="mu")
+            nc.scalar.activation(out=un[u]["mu"][:], in_=un[u]["acc"][:], func=ACT.Copy, scale=1.0 / C)
+
+        def xbank(u, g):
+            xb = ps_x.tile([P, 2 * J], F32, name="xb").rearrange("p (e j) -> p e j", e=2)
+            un[u][("xb", g)] = xb
+            for e in range(2):
+                mx(xb[:, e, :], u, 2 * g + e, True, True)
+            if g == XB - 1:
+                st["mx_done"] = u + 1
+
+        def sub(u, g):
+            un[u]["t"] = t_fixed[u % 2]
+            nc.vector.tensor_tensor(
+                out=un[u]["t"][:, 2 * g:2 * g + 2, :], in0=un[u][("xb", g)][:],
+                in1=un[u]["mu"][:].unsqueeze(1).to_broadcast([P, 2, J]), op=ALU.subtract,
+            )
+
+        def square(u, h):
+            if h == 0:
+                un[u]["sq"] = sqp.tile([P, C, J], F32, name="sq")
+            nc.scalar.activation(
+                out=un[u]["sq"][:, 4 * h:4 * h + 4, :], in_=un[u]["t"][:, 4 * h:4 * h + 4, :], func=ACT.Square)
+
+        def chain(u, jb, cs):
+            if jb == 0 and cs[0] == 0:
+                un[u]["q_t"] = ps_stat.tile([P, J], F32, name="stat")
+            cols = slice(jb * P, (jb + 1) * P)
+            for c in cs:
+                nc.tensor.matmul(
+                    out=un[u]["q_t"][:, cols], lhsT=un[u]["sq"][:, c, cols], rhs=ident[:],
+                    is_transpose=True, start=(c == 0), stop=(c == C - 1),
                 )
-            sq = sqp.tile([P, C, J], F32, name="sq")
-            for g in range(4):
-                nc.scalar.activation(out=sq[:, 4 * g:4 * g + 4, :], in_=t[:, 4 * g:4 * g + 4, :], func=ACT.Square)
-            q_t = ps_q.tile([P, J], F32, name="q_t")
+
+        def sigma(u):
+            un[u]["sig_t"] = small.tile([P, J], F32, name="sig_t")
+            nc.scalar.activation(
+                out=un[u]["sig_t"][:], in_=un[u]["q_t"][:], func=ACT.Sqrt, scale=1.0 / C, bias=eps[:])
+
+        def recip(u):
+            un[u]["r_t"] = small.tile([P, J], F32, name="r_t")
+            nc.vector.reciprocal(out=un[u]["r_t"][:], in_=un[u]["sig_t"][:])
+
+        def rback(u):
+            un[u]["r"] = ps_r.tile([P, J], F32, name="r")
             for jb in range(J // P):
                 cols = slice(jb * P, (jb + 1) * P)
-                for c in range(C):
-                    nc.tensor.matmul(
-                        out=q_t[:, cols], lhsT=sq[:, c, cols], rhs=ident[:],
-                        is_transpose=True, start=(c == 0), stop=(c == C - 1),
-                    )
-            sig_t = small.tile([P, J], F32, name="sig_t")
-            nc.scalar.activation(out=sig_t[:], in_=q_t[:], func=ACT.Sqrt, scale=1.0 / C, bias=eps[:])
-            r_t = small.tile([P, J], F32, name="r_t")
-            nc.vector.reciprocal(out=r_t[:], in_=sig_t[:])
-            r = ps_r.tile([P, J], F32, name="r")
-            for jb in range(J // P):
-                cols = slice(jb * P, (jb + 1) * P)
-                nc.tensor.transpose(r[:, cols], r_t[:, cols], ident[:])
-            for c in range(C):
-                nc.vector.scalar_tensor_tensor(
-                    out=t[:, c, :], in0=t[:, c, :], scalar=w_f[:, c:c + 1], in1=r[:],
-                    op0=ALU.mult, op1=ALU.mult,
-                )
-            o = op.tile([P, J, C], F32, name="o")
-            for g in range(4):
-                nc.vector.tensor_tensor(
-                    out=o[:, :, 4 * g:4 * g + 4],
-                    in0=t[:, 4 * g:4 * g + 4, :].rearrange("p c j -> p j c"),
-                    in1=b_f[:, 4 * g:4 * g + 4].unsqueeze(1).to_broadcast([P, J, 4]),
-                    op=ALU.add,
-                )
-            nc.sync.dma_start(
+                nc.tensor.transpose(un[u]["r"][:, cols], un[u]["r_t"][:, cols], ident[:])
+
+        def scale(u, c):
+            t = un[u]["t"]
+            nc.vector.scalar_tensor_tensor(
+                out=t[:, c, :], in0=t[:, c, :], scalar=w_f[:, c:c + 1], in1=un[u]["r"][:],
+                op0=ALU.mult, op1=ALU.mult,
+            )
+
+        def bias(u, g, engine):
+            if g == 0:
+                un[u]["o"] = op.tile([P, J, C], F32, name="o")
+            engine.tensor_tensor(
+                out=un[u]["o"][:, :, 4 * g:4 * g + 4],
+                in0=un[u]["t"][:, 4 * g:4 * g + 4, :].rearrange("p c j -> p j c"),
+                in1=b_f[:, 4 * g:4 * g + 4].unsqueeze(1).to_broadcast([P, J, 4]),
+                op=ALU.add,
+            )
+
+        def store(u):
+            jp, it = u // 2, u % 2
+            nc.gpsimd.dma_start(
                 out=out[it * P:(it + 1) * P, jp * J:(jp + 1) * J, :].rearrange("i j c -> i (j c)"),
-                in_=o[:].rearrange("p j c -> p (j c)"),
+                in_=un[u]["o"][:].rearrange("p j c -> p (j c)"),
             )
 
-        prep_a(0)
-        cur = new_b()
-        prep_b(cur[0], cur[1], 0, 0, 4)
-        prep_b(cur[0], cur[1], 0, 1, 4)
-        prep_a(1)
-        for jp in range(BJ // J):
-            nxt = None
-            if jp + 1 < BJ // J:
-                nxt = new_b()
-            unit(0, jp, cur[0], cur[1])
-            if nxt is not None:
-                prep_b(nxt[0], nxt[1], jp + 1, 0, 0)
-            unit(1, jp, cur[0], cur[1])
-            if nxt is not None:
-                prep_b(nxt[0], nxt[1], jp + 1, 1, 0)
-            cur = nxt
+        def s_exits(n):
+            for i in range(n):
+                leave(False)
+                top_up()
+
+        def v_exits(n):
+            for i in range(n):
+                leave(True)
+                top_up()
+
+        def codes_ready(u):
+            last = max(TILES.index(("b", 2 * (u // 2) + 1)), TILES.index(("a", u % 2)))
+            return st["quantised"] > last
+
+        def finish(p):
+            last = p == NU - 1
+            for c in range(C):
+                scale(p, c)
+                if c % 4 == 3 and not (last and c // 4 >= 2):
+                    bias(p, c // 4, nc.gpsimd)
+            if last:
+                bias(p, 2, nc.vector)
+                bias(p, 3, nc.vector)
+            store(p)
+
+        def period(p):
+            nxt, nn = p + 1, p + 2
+            if p >= 0:
+                rback(p)
+            for i in range(S_A[p + 1]):
+                leave(False)
+            early = nn < NU and codes_ready(nn)
+            if nxt < NU:
+                for g in range(XB):
+                    sub(nxt, g)
+                    if g + XRING < XB:
+                        xbank(nxt, g + XRING)
+                    if early:
+                        total(nn, [2 * g, 2 * g + 1])
+                    if g % 2 == 1:
+                        square(nxt, g // 2)
+                if early:
+                    mean(nn)
+                    for g in range(XRING):
+                        xbank(nn, g)
+                top_up()
+                chain(nxt, 0, list(range(C)))
+                chain(nxt, 1, list(range(C)))
+            s_exits(S_B[p + 1])
+            if nxt < NU:
+                sigma(nxt)
+            if p >= 0 and early:
+                finish(p)
+            v_exits(V_X[p + 1])
+            s_exits(S_C[p + 1])
+            quantise_ready()
+            if nn < NU and not early:
+                need(nn)
+                total(nn, list(range(C)))
+            if p >= 0 and not early:
+                finish(p)
+            s_exits(S_D[p + 1])
+            if nn < NU and not early:
+                mean(nn)
+                for g in range(XRING):
+                    xbank(nn, g)
+            s_exits(S_E[p + 1])
+            quantise_ready()
+            if nxt < NU:
+                recip(nxt)
+
+        nc.scalar.dma_start(out=w_bf[:], in_=ln2_w.partition_broadcast(P))
+        nc.scalar.dma_start(out=b_bf[:], in_=ln2_b.partition_broadcast(P))
+        load(0)
+        load(1)
+        load(2)
+        nc.vector.tensor_copy(out=w_f[:], in_=w_bf[:])
+        nc.vector.tensor_copy(out=b_f[:], in_=b_bf[:])
+        top_up()
+        for k in range(WARM):
+            leave(k % WARM_OF < WARM_V)
+            top_up()
+            if k % CP == 2:
+                quantise_ready()
+        need(0)
+        total(0, list(range(C)))
+        mean(0)
+        for g in range(XRING):
+            xbank(0, g)
+        for p in range(-1, NU):
+            period(p)

@@ -30,12 +30,13 @@ TILES = [("a", 0), ("b", 0), ("b", 1), ("a", 1)] + [("b", n) for n in range(2, B
 WARM = 24
 WARM_V = 2
 WARM_OF = 4
-S_A = [1,2,2,1,4,6,3,1,3]
-S_B = [1,5,2,1,3,2,0,4,2]
-S_C = [0,1,4,1,3,5,3,3,2]
-S_D = [3,3,0,3,0,0,4,2,0]
-V_X = [3,4,1,1,0,0,3,0,1]
-S_E = [0,2,0,1,0,1,3,1,1]
+S_A = [2,1,2,1,3,6,1,0,1]
+S_B = [0,5,2,3,8,2,0,4,1]
+S_C = [0,3,4,1,0,3,4,3,3]
+S_D = [3,4,0,3,0,1,6,0,1]
+V_X = [5,4,1,1,0,4,3,2,2]
+S_E = [0,1,0,2,1,1,3,6,0]
+G32 = [7,5,8,6,6,5,6,4,3]
 
 
 def tile_trianglemultiplication_pa_t_kernel(tc, a_proj, b_proj, ln2_w, ln2_b, out):
@@ -206,13 +207,12 @@ def tile_trianglemultiplication_pa_t_kernel(tc, a_proj, b_proj, ln2_w, ln2_b, ou
                 )
 
         def sigma(u):
-            un[u]["sig_t"] = small.tile([P, J], F32, name="sig_t")
+            un[u]["r_t"] = small.tile([P, J], F32, name="r_t")
             nc.scalar.activation(
-                out=un[u]["sig_t"][:], in_=un[u]["q_t"][:], func=ACT.Sqrt, scale=1.0 / C, bias=eps[:])
+                out=un[u]["r_t"][:], in_=un[u]["q_t"][:], func=ACT.Abs_reciprocal_sqrt, scale=1.0 / C, bias=eps[:])
 
         def recip(u):
-            un[u]["r_t"] = small.tile([P, J], F32, name="r_t")
-            nc.vector.reciprocal(out=un[u]["r_t"][:], in_=un[u]["sig_t"][:])
+            return
 
         def rback(u):
             un[u]["r"] = ps_r.tile([P, J], F32, name="r")
@@ -227,13 +227,13 @@ def tile_trianglemultiplication_pa_t_kernel(tc, a_proj, b_proj, ln2_w, ln2_b, ou
                 op0=ALU.mult, op1=ALU.mult,
             )
 
-        def bias(u, g, engine):
-            if g == 0:
+        def bias(u, g, engine, j0, j1):
+            if "o" not in un[u]:
                 un[u]["o"] = op.tile([P, J, C], F32, name="o")
             engine.tensor_tensor(
-                out=un[u]["o"][:, :, 4 * g:4 * g + 4],
-                in0=un[u]["t"][:, 4 * g:4 * g + 4, :].rearrange("p c j -> p j c"),
-                in1=b_f[:, 4 * g:4 * g + 4].unsqueeze(1).to_broadcast([P, J, 4]),
+                out=un[u]["o"][:, j0:j1, 4 * g:4 * g + 4],
+                in0=un[u]["t"][:, 4 * g:4 * g + 4, j0:j1].rearrange("p c j -> p j c"),
+                in1=b_f[:, 4 * g:4 * g + 4].unsqueeze(1).to_broadcast([P, j1 - j0, 4]),
                 op=ALU.add,
             )
 
@@ -259,14 +259,14 @@ def tile_trianglemultiplication_pa_t_kernel(tc, a_proj, b_proj, ln2_w, ln2_b, ou
             return st["quantised"] > last
 
         def finish(p):
-            last = p == NU - 1
+            ng = 32 * G32[p + 1]
             for c in range(C):
                 scale(p, c)
-                if c % 4 == 3 and not (last and c // 4 >= 2):
-                    bias(p, c // 4, nc.gpsimd)
-            if last:
-                bias(p, 2, nc.vector)
-                bias(p, 3, nc.vector)
+                if c % 4 == 3 and ng > 0:
+                    bias(p, c // 4, nc.gpsimd, 0, ng)
+            if ng < J:
+                for g in range(4):
+                    bias(p, g, nc.vector, ng, J)
             store(p)
 
         def period(p):

@@ -18,25 +18,19 @@ BI = 256
 BJ = 1024
 PACK = 4
 CP = C // 2
-J = 256
+NI = BI // P
+NU = BJ // P
 EPS = 1e-5
 FLOPS = 2 * C * BI * BJ * K
 
-NU = (BI // P) * (BJ // J)
 RING = 4
 XRING = 2
-XB = C // 2
-TILES = [("a", 0), ("b", 0), ("b", 1), ("a", 1)] + [("b", n) for n in range(2, BJ // P)]
-WARM = 24
-WARM_V = 2
-WARM_OF = 4
-S_A = [2,1,2,1,3,6,1,0,1]
-S_B = [0,5,2,3,8,2,0,4,1]
-S_C = [0,3,4,1,0,3,4,3,3]
-S_D = [3,4,0,3,0,1,6,0,1]
-V_X = [5,4,1,1,0,4,3,2,2]
-S_E = [0,1,0,2,1,1,3,6,0]
-G32 = [7,5,8,6,6,5,6,4,3]
+XB = NI * C // 4
+NT = NI + NU
+WARM = 3 * CP
+JG = 96
+AHEAD = 3
+FIRST = -1
 
 
 def tile_trianglemultiplication_pa_t_kernel(tc, a_proj, b_proj, ln2_w, ln2_b, out):
@@ -63,26 +57,29 @@ def tile_trianglemultiplication_pa_t_kernel(tc, a_proj, b_proj, ln2_w, ln2_b, ou
         b_f = const.tile([P, C], F32, name="b_f")
         eps = const.tile([P, 1], F32, name="eps")
         nc.vector.memset(eps[:], EPS)
-        a_codes = const.tile([P, BI // P, C, P], U32, name="a_codes", align_bytes=64)
-        a_scales = const.tile([P, BI // P, C, P], U8, name="a_scales", align_bytes=64)
-        t_fixed = [const.tile([P, C, J], F32, name="t0"), const.tile([P, C, J], F32, name="t1")]
+        a_codes = const.tile([P, NI, C, P], U32, name="a_codes", align_bytes=64)
+        a_scales = const.tile([P, NI, C, P], U8, name="a_scales", align_bytes=64)
+        t_fixed = [const.tile([P, NI, C, P], F32, name="t0"), const.tile([P, NI, C, P], F32, name="t1")]
 
-        st = {"loaded": 0, "filled": 0, "exited": 0, "quantised": 0, "mx_done": 0}
+        st = {"loaded": 0, "filled": 0, "exited": 0, "quantised": 0}
         nat = {}
         grouped = {}
         banks = {}
-        pair = {}
+        bq = {}
         un = [dict() for u in range(NU)]
 
         def load(n):
-            kind, idx = TILES[n]
-            src = a_proj if kind == "a" else b_proj
+            src = a_proj if n < NI else b_proj
+            r0 = (n if n < NI else n - NI) * P
             nat[n] = natp.tile([P, K * C], BF16, name="nat")
-            nc.sync.dma_start(out=nat[n][:], in_=src[idx * P:(idx + 1) * P, :, :].rearrange("r k c -> r (k c)"))
+            nc.sync.dma_start(out=nat[n][:], in_=src[r0:r0 + P, :, :].rearrange("r k c -> r (k c)"))
             st["loaded"] = n + 1
 
         def fill():
             k = st["filled"]
+            if k >= CP * NT:
+                return
+            assert k - st["exited"] < (RING + XRING if k < WARM else RING)
             n, w = k // CP, k % CP
             words = nat[n][:].bitcast(F32).rearrange("p (q t w) -> p q t w", t=PACK, w=CP)
             if k < WARM and k % 3 == 2:
@@ -92,20 +89,19 @@ def tile_trianglemultiplication_pa_t_kernel(tc, a_proj, b_proj, ln2_w, ln2_b, ou
             for t in range(PACK):
                 nc.tensor.transpose(banks[k][:, t * P:(t + 1) * P], words[:, :, t, w], ident[:])
             st["filled"] = k + 1
-            if w == CP - 1 and st["loaded"] < len(TILES):
+            if w == CP - 1 and st["loaded"] < NT:
                 load(st["loaded"])
 
         def top_up():
             ring = RING + XRING if st["filled"] < WARM else RING
-            while st["filled"] < min(st["exited"] + ring, CP * len(TILES)):
+            while st["filled"] < min(st["exited"] + ring, CP * NT):
                 fill()
 
         def leave(on_vector):
             k = st["exited"]
-            if k >= CP * len(TILES):
+            if k >= CP * NT:
                 return
-            if k >= st["filled"]:
-                top_up()
+            assert k < st["filled"]
             n, w = k // CP, k % CP
             if w == 0:
                 grouped[n] = grp.tile([P, C, P, PACK], BF16, name="grouped", align_bytes=64)
@@ -118,202 +114,163 @@ def tile_trianglemultiplication_pa_t_kernel(tc, a_proj, b_proj, ln2_w, ln2_b, ou
             st["exited"] = k + 1
 
         def quantise(n):
-            kind, idx = TILES[n]
-            if kind == "b" and idx % 2 == 0:
-                pair[idx // 2] = (
-                    bqp.tile([P, C, J], U32, name="b_codes", align_bytes=64),
-                    bqp.tile([P, C, J], U8, name="b_scales", align_bytes=64),
+            if n < NI:
+                codes, scales = a_codes[:, n, :, :], a_scales[:, n, :, :]
+            else:
+                bq[n - NI] = (
+                    bqp.tile([P, C, P], U32, name="b_codes", align_bytes=64),
+                    bqp.tile([P, C, P], U8, name="b_scales", align_bytes=64),
                 )
-            for c in range(C):
-                if kind == "a":
-                    codes, scales = a_codes[:, idx, c, :], a_scales[:, idx, c, :]
-                else:
-                    h = idx % 2
-                    codes = pair[idx // 2][0][:, c, h * P:(h + 1) * P]
-                    scales = pair[idx // 2][1][:, c, h * P:(h + 1) * P]
+                codes, scales = bq[n - NI][0][:], bq[n - NI][1][:]
+            for h in range(2):
+                cs = slice(h * CP, (h + 1) * CP)
                 nc.vector.quantize_mx(
-                    out=codes.bitcast(FP8X4), scales=scales,
-                    in_=grouped[n][:, c, :, :].rearrange("p r t -> p (r t)"),
+                    out=codes[:, cs, :].rearrange("p c r -> p (c r)").bitcast(FP8X4),
+                    scales=scales[:, cs, :].rearrange("p c r -> p (c r)"),
+                    in_=grouped[n][:, cs, :, :].rearrange("p c r t -> p (c r t)"),
                 )
             st["quantised"] = n + 1
 
-        def may_quantise(n):
-            kind, idx = TILES[n]
-            if st["exited"] < CP * (n + 1):
-                return False
-            return kind == "a" or idx // 2 < 2 or st["mx_done"] >= 2 * (idx // 2 - 2) + 2
-
-        def quantise_ready():
-            while st["quantised"] < len(TILES) and may_quantise(st["quantised"]):
+        def prepare(n):
+            assert st["exited"] >= CP * (n + 1)
+            while st["quantised"] <= n:
                 quantise(st["quantised"])
 
-        def need(u):
-            last = TILES.index(("b", 2 * (u // 2) + 1))
-            last = max(last, TILES.index(("a", u % 2)))
-            while st["exited"] < CP * (last + 1):
-                leave(st["exited"] % 2 == 0)
-                top_up()
-            quantise_ready()
-            assert st["quantised"] > last
-
-        def mx(dst, u, c, start, stop):
-            codes, scales = pair[u // 2]
+        def mx(dst, u, it, c, start, stop):
             nc.tensor.matmul_mx(
                 out=dst,
-                lhsT=a_codes[:, u % 2, c, :].bitcast(FP8X4), lhsT_scale=a_scales[:, u % 2, c, :],
-                rhs=codes[:, c, :].bitcast(FP8X4), rhs_scale=scales[:, c, :],
+                lhsT=a_codes[:, it, c, :].bitcast(FP8X4), lhsT_scale=a_scales[:, it, c, :],
+                rhs=bq[u][0][:, c, :].bitcast(FP8X4), rhs_scale=bq[u][1][:, c, :],
                 start=start, stop=stop,
             )
 
-        def total(u, cs):
-            if cs[0] == 0:
-                un[u]["acc"] = ps_stat.tile([P, J], F32, name="stat")
-            for c in cs:
-                mx(un[u]["acc"][:], u, c, c == 0, c == C - 1)
+        def total(u):
+            un[u]["acc"] = ps_stat.tile([P, NI, P], F32, name="stat")
+            for it in range(NI):
+                for c in range(C):
+                    mx(un[u]["acc"][:, it, :], u, it, c, c == 0, c == C - 1)
 
         def mean(u):
-            un[u]["mu"] = small.tile([P, J], F32, name="mu")
+            un[u]["mu"] = small.tile([P, NI, P], F32, name="mu")
             nc.scalar.activation(out=un[u]["mu"][:], in_=un[u]["acc"][:], func=ACT.Copy, scale=1.0 / C)
 
-        def xbank(u, g):
-            xb = ps_x.tile([P, 2 * J], F32, name="xb").rearrange("p (e j) -> p e j", e=2)
-            un[u][("xb", g)] = xb
-            for e in range(2):
-                mx(xb[:, e, :], u, 2 * g + e, True, True)
-            if g == XB - 1:
-                st["mx_done"] = u + 1
+        def xbank(u, b):
+            it, g = b // 4, b % 4
+            xb = ps_x.tile([P, PACK * P], F32, name="xb").rearrange("p (c j) -> p c j", c=4)
+            un[u][("xb", b)] = xb
+            for e in range(4):
+                mx(xb[:, e, :], u, it, 4 * g + e, True, True)
 
-        def sub(u, g):
+        def sub(u, b):
+            it, g = b // 4, b % 4
             un[u]["t"] = t_fixed[u % 2]
             nc.vector.tensor_tensor(
-                out=un[u]["t"][:, 2 * g:2 * g + 2, :], in0=un[u][("xb", g)][:],
-                in1=un[u]["mu"][:].unsqueeze(1).to_broadcast([P, 2, J]), op=ALU.subtract,
+                out=un[u]["t"][:, it, 4 * g:4 * g + 4, :], in0=un[u][("xb", b)],
+                in1=un[u]["mu"][:, it, :].unsqueeze(1).to_broadcast([P, 4, P]), op=ALU.subtract,
             )
 
         def square(u, h):
             if h == 0:
-                un[u]["sq"] = sqp.tile([P, C, J], F32, name="sq")
-            nc.scalar.activation(
-                out=un[u]["sq"][:, 4 * h:4 * h + 4, :], in_=un[u]["t"][:, 4 * h:4 * h + 4, :], func=ACT.Square)
+                un[u]["sq"] = sqp.tile([P, NI, C, P], F32, name="sq")
+            it, cs = h // 2, slice((h % 2) * CP, (h % 2 + 1) * CP)
+            nc.scalar.activation(out=un[u]["sq"][:, it, cs, :], in_=un[u]["t"][:, it, cs, :], func=ACT.Square)
 
-        def chain(u, jb, cs):
-            if jb == 0 and cs[0] == 0:
-                un[u]["q_t"] = ps_stat.tile([P, J], F32, name="stat")
-            cols = slice(jb * P, (jb + 1) * P)
-            for c in cs:
+        def chain(u, it):
+            if it == 0:
+                un[u]["q_t"] = ps_stat.tile([P, NI, P], F32, name="stat")
+            for c in range(C):
                 nc.tensor.matmul(
-                    out=un[u]["q_t"][:, cols], lhsT=un[u]["sq"][:, c, cols], rhs=ident[:],
+                    out=un[u]["q_t"][:, it, :], lhsT=un[u]["sq"][:, it, c, :], rhs=ident[:],
                     is_transpose=True, start=(c == 0), stop=(c == C - 1),
                 )
 
         def sigma(u):
-            un[u]["r_t"] = small.tile([P, J], F32, name="r_t")
+            un[u]["r_t"] = small.tile([P, NI, P], F32, name="r_t")
             nc.scalar.activation(
                 out=un[u]["r_t"][:], in_=un[u]["q_t"][:], func=ACT.Abs_reciprocal_sqrt, scale=1.0 / C, bias=eps[:])
 
-        def recip(u):
-            return
-
         def rback(u):
-            un[u]["r"] = ps_r.tile([P, J], F32, name="r")
-            for jb in range(J // P):
-                cols = slice(jb * P, (jb + 1) * P)
-                nc.tensor.transpose(un[u]["r"][:, cols], un[u]["r_t"][:, cols], ident[:])
+            un[u]["r"] = ps_r.tile([P, NI, P], F32, name="r")
+            for it in range(NI):
+                nc.tensor.transpose(un[u]["r"][:, it, :], un[u]["r_t"][:, it, :], ident[:])
 
         def scale(u, c):
             t = un[u]["t"]
             nc.vector.scalar_tensor_tensor(
-                out=t[:, c, :], in0=t[:, c, :], scalar=w_f[:, c:c + 1], in1=un[u]["r"][:],
+                out=t[:, :, c, :], in0=t[:, :, c, :], scalar=w_f[:, c:c + 1], in1=un[u]["r"][:],
                 op0=ALU.mult, op1=ALU.mult,
             )
 
         def bias(u, g, engine, j0, j1):
             if "o" not in un[u]:
-                un[u]["o"] = op.tile([P, J, C], F32, name="o")
+                un[u]["o"] = op.tile([P, NI, P, C], F32, name="o")
             engine.tensor_tensor(
-                out=un[u]["o"][:, j0:j1, 4 * g:4 * g + 4],
-                in0=un[u]["t"][:, 4 * g:4 * g + 4, j0:j1].rearrange("p c j -> p j c"),
-                in1=b_f[:, 4 * g:4 * g + 4].unsqueeze(1).to_broadcast([P, j1 - j0, 4]),
+                out=un[u]["o"][:, :, j0:j1, 4 * g:4 * g + 4],
+                in0=un[u]["t"][:, :, 4 * g:4 * g + 4, j0:j1].rearrange("p i c j -> p i j c"),
+                in1=b_f[:, 4 * g:4 * g + 4].unsqueeze(1).unsqueeze(1).to_broadcast([P, NI, j1 - j0, 4]),
                 op=ALU.add,
             )
 
         def store(u):
-            jp, it = u // 2, u % 2
             nc.gpsimd.dma_start(
-                out=out[it * P:(it + 1) * P, jp * J:(jp + 1) * J, :].rearrange("i j c -> i (j c)"),
-                in_=un[u]["o"][:].rearrange("p j c -> p (j c)"),
+                out=out[:, u * P:(u + 1) * P, :].rearrange("(i p) j c -> p i (j c)", p=P),
+                in_=un[u]["o"][:].rearrange("p i j c -> p i (j c)"),
             )
-
-        def s_exits(n):
-            for i in range(n):
-                leave(False)
-                top_up()
-
-        def v_exits(n):
-            for i in range(n):
-                leave(True)
-                top_up()
-
-        def codes_ready(u):
-            last = max(TILES.index(("b", 2 * (u // 2) + 1)), TILES.index(("a", u % 2)))
-            return st["quantised"] > last
-
-        def finish(p):
-            ng = 32 * G32[p + 1]
-            for c in range(C):
-                scale(p, c)
-                if c % 4 == 3 and ng > 0:
-                    bias(p, c // 4, nc.gpsimd, 0, ng)
-            if ng < J:
-                for g in range(4):
-                    bias(p, g, nc.vector, ng, J)
-            store(p)
 
         def period(p):
             nxt, nn = p + 1, p + 2
-            if p >= 0:
-                rback(p)
-            for i in range(S_A[p + 1]):
-                leave(False)
-            early = nn < NU and codes_ready(nn)
-            if nxt < NU:
-                for g in range(XB):
-                    sub(nxt, g)
-                    if g + XRING < XB:
-                        xbank(nxt, g + XRING)
-                    if early:
-                        total(nn, [2 * g, 2 * g + 1])
-                    if g % 2 == 1:
-                        square(nxt, g // 2)
-                if early:
-                    mean(nn)
-                    for g in range(XRING):
-                        xbank(nn, g)
-                top_up()
-                chain(nxt, 0, list(range(C)))
-                chain(nxt, 1, list(range(C)))
-            s_exits(S_B[p + 1])
-            if nxt < NU:
+            helper = p < 0
+            jg = JG if p < NU - 1 else P // 2
+            if 0 <= nxt < NU:
+                total(nxt)
+            if 0 <= p < NU:
+                for c in range(C):
+                    scale(p, c)
+                    if c % 4 == 3:
+                        bias(p, c // 4, nc.gpsimd, 0, jg)
+            leave(helper)
+            leave(False)
+            fill()
+            fill()
+            leave(helper)
+            if 0 <= nxt < NU:
+                mean(nxt)
+            fill()
+            leave(False)
+            leave(helper)
+            if 0 <= nxt < NU:
+                for b in range(XB):
+                    sub(nxt, b)
+                    if b + XRING < XB:
+                        xbank(nxt, b + XRING)
+                    if b % 2 == 1:
+                        square(nxt, b // 2)
+            if 0 <= p < NU:
+                for g in range(4):
+                    bias(p, g, nc.vector, jg, P)
+                store(p)
+            if 0 <= nxt < NU:
+                chain(nxt, 0)
+            fill()
+            if 0 <= nxt < NU:
+                chain(nxt, 1)
+            fill()
+            leave(False)
+            if 0 <= nxt < NU:
                 sigma(nxt)
-            if p >= 0 and early:
-                finish(p)
-            v_exits(V_X[p + 1])
-            s_exits(S_C[p + 1])
-            quantise_ready()
-            if nn < NU and not early:
-                need(nn)
-                total(nn, list(range(C)))
-            if p >= 0 and not early:
-                finish(p)
-            s_exits(S_D[p + 1])
-            if nn < NU and not early:
-                mean(nn)
-                for g in range(XRING):
-                    xbank(nn, g)
-            s_exits(S_E[p + 1])
-            quantise_ready()
-            if nxt < NU:
-                recip(nxt)
+            fill()
+            leave(False)
+            leave(False)
+            if st["quantised"] < NT:
+                assert st["exited"] >= min(CP * (st["quantised"] + 1), CP * NT)
+                quantise(st["quantised"])
+            if 0 <= nxt < NU:
+                rback(nxt)
+            if 0 <= nn < NU:
+                for b in range(XRING):
+                    xbank(nn, b)
+            fill()
+            fill()
 
         nc.scalar.dma_start(out=w_bf[:], in_=ln2_w.partition_broadcast(P))
         nc.scalar.dma_start(out=b_bf[:], in_=ln2_b.partition_broadcast(P))
@@ -324,14 +281,15 @@ def tile_trianglemultiplication_pa_t_kernel(tc, a_proj, b_proj, ln2_w, ln2_b, ou
         nc.vector.tensor_copy(out=b_f[:], in_=b_bf[:])
         top_up()
         for k in range(WARM):
-            leave(k % WARM_OF < WARM_V)
+            leave(k % 2 == 0)
             top_up()
-            if k % CP == 2:
-                quantise_ready()
-        need(0)
-        total(0, list(range(C)))
-        mean(0)
-        for g in range(XRING):
-            xbank(0, g)
-        for p in range(-1, NU):
+            if k % CP == 2 and k > CP:
+                quantise(st["quantised"])
+        quantise(st["quantised"])
+        for k in range(AHEAD):
+            leave(k % 2 == 0)
+            fill()
+        for b in range(XRING):
+            xbank(0, b)
+        for p in range(FIRST, NU):
             period(p)

@@ -23,8 +23,8 @@ NU = BJ // P
 EPS = 1e-5
 FLOPS = 2 * C * BI * BJ * K
 
-RING = 4
-XRING = 2
+RING = 3
+XRING = 3
 XB = NI * C // 4
 NT = NI + NU
 WARM = 3 * CP
@@ -82,7 +82,7 @@ def tile_trianglemultiplication_pa_t_kernel(tc, a_proj, b_proj, ln2_w, ln2_b, ou
             assert k - st["exited"] < (RING + XRING if k < WARM else RING)
             n, w = k // CP, k % CP
             words = nat[n][:].bitcast(F32).rearrange("p (q t w) -> p q t w", t=PACK, w=CP)
-            if k < WARM and k % 3 == 2:
+            if k < WARM and k % 2 == 1:
                 banks[k] = ps_x.tile([P, PACK * P], F32, name="xb")
             else:
                 banks[k] = ps_tr.tile([P, PACK * P], F32, name="bank")
@@ -212,7 +212,7 @@ def tile_trianglemultiplication_pa_t_kernel(tc, a_proj, b_proj, ln2_w, ln2_b, ou
             )
 
         def store(u):
-            nc.gpsimd.dma_start(
+            nc.sync.dma_start(
                 out=out[:, u * P:(u + 1) * P, :].rearrange("(i p) j c -> p i (j c)", p=P),
                 in_=un[u]["o"][:].rearrange("p i j c -> p i (j c)"),
             )
@@ -281,7 +281,7 @@ def tile_trianglemultiplication_pa_t_kernel(tc, a_proj, b_proj, ln2_w, ln2_b, ou
         nc.vector.tensor_copy(out=b_f[:], in_=b_bf[:])
         top_up()
         for k in range(WARM):
-            leave(k % 2 == 0)
+            leave(k % 8 in (1, 4, 6))
             top_up()
             if k % CP == 2 and k > CP:
                 quantise(st["quantised"])

@@ -28,7 +28,7 @@ XRING = 3
 XB = NI * C // 4
 NT = NI + NU
 WARM = 3 * CP
-JG = 96
+JG = 64
 AHEAD = 3
 FIRST = -1
 
@@ -220,14 +220,13 @@ def tile_trianglemultiplication_pa_t_kernel(tc, a_proj, b_proj, ln2_w, ln2_b, ou
         def period(p):
             nxt, nn = p + 1, p + 2
             helper = p < 0
-            jg = JG if p < NU - 1 else P // 2
             if 0 <= nxt < NU:
                 total(nxt)
             if 0 <= p < NU:
                 for c in range(C):
                     scale(p, c)
                     if c % 4 == 3:
-                        bias(p, c // 4, nc.gpsimd, 0, jg)
+                        bias(p, c // 4, nc.gpsimd, 0, JG)
             leave(helper)
             leave(False)
             fill()
@@ -237,7 +236,7 @@ def tile_trianglemultiplication_pa_t_kernel(tc, a_proj, b_proj, ln2_w, ln2_b, ou
                 mean(nxt)
             fill()
             leave(False)
-            leave(helper)
+            leave(False)
             if 0 <= nxt < NU:
                 for b in range(XB):
                     sub(nxt, b)
@@ -247,7 +246,7 @@ def tile_trianglemultiplication_pa_t_kernel(tc, a_proj, b_proj, ln2_w, ln2_b, ou
                         square(nxt, b // 2)
             if 0 <= p < NU:
                 for g in range(4):
-                    bias(p, g, nc.vector, jg, P)
+                    bias(p, g, nc.vector, JG, P)
                 store(p)
             if 0 <= nxt < NU:
                 chain(nxt, 0)
@@ -280,15 +279,11 @@ def tile_trianglemultiplication_pa_t_kernel(tc, a_proj, b_proj, ln2_w, ln2_b, ou
         nc.vector.tensor_copy(out=w_f[:], in_=w_bf[:])
         nc.vector.tensor_copy(out=b_f[:], in_=b_bf[:])
         top_up()
-        for k in range(WARM):
+        for k in range(WARM + AHEAD):
             leave(k % 8 in (1, 4, 6))
             top_up()
-            if k % CP == 2 and k > CP:
+            if k % CP == AHEAD - 1 and k > CP:
                 quantise(st["quantised"])
-        quantise(st["quantised"])
-        for k in range(AHEAD):
-            leave(k % 2 == 0)
-            fill()
         for b in range(XRING):
             xbank(0, b)
         for p in range(FIRST, NU):

@@ -258,11 +258,11 @@ def tile_trianglemultiplication_pa_t_kernel(tc, a_proj, b_proj, ln2_w, ln2_b, ou
             if 0 <= nxt < NU:
                 sigma(nxt)
             fill()
-            leave(False)
-            leave(False)
             if st["quantised"] < NT:
                 assert st["exited"] >= min(CP * (st["quantised"] + 1), CP * NT)
                 quantise(st["quantised"])
+            leave(True)
+            leave(False)
             if 0 <= nxt < NU:
                 rback(nxt)
             if 0 <= nn < NU:

@@ -31,6 +31,7 @@ WARM = 3 * CP
 JG = 64
 AHEAD = 3
 FIRST = -1
+SPLIT = 1
 
 
 def tile_trianglemultiplication_pa_t_kernel(tc, a_proj, b_proj, ln2_w, ln2_b, out):
@@ -72,7 +73,13 @@ def tile_trianglemultiplication_pa_t_kernel(tc, a_proj, b_proj, ln2_w, ln2_b, ou
             src = a_proj if n < NI else b_proj
             r0 = (n if n < NI else n - NI) * P
             nat[n] = natp.tile([P, K * C], BF16, name="nat")
-            nc.sync.dma_start(out=nat[n][:], in_=src[r0:r0 + P, :, :].rearrange("r k c -> r (k c)"))
+            pieces = PACK if n < SPLIT else 1
+            kk = K // pieces
+            for i in range(pieces):
+                nc.sync.dma_start(
+                    out=nat[n][:, i * kk * C:(i + 1) * kk * C],
+                    in_=src[r0:r0 + P, i * kk:(i + 1) * kk, :].rearrange("r k c -> r (k c)"),
+                )
             st["loaded"] = n + 1
 
         def fill():
@@ -81,7 +88,7 @@ def tile_trianglemultiplication_pa_t_kernel(tc, a_proj, b_proj, ln2_w, ln2_b, ou
                 return
             assert k - st["exited"] < (RING + XRING if k < WARM else RING)
             n, w = k // CP, k % CP
-            words = nat[n][:].bitcast(F32).rearrange("p (q t w) -> p q t w", t=PACK, w=CP)
+            words = nat[n][:].bitcast(F32).rearrange("p (t q w) -> p q t w", t=PACK, w=CP)
             if k < WARM and k % 2 == 1:
                 banks[k] = ps_x.tile([P, PACK * P], F32, name="xb")
             else:
@@ -271,19 +278,28 @@ def tile_trianglemultiplication_pa_t_kernel(tc, a_proj, b_proj, ln2_w, ln2_b, ou
             fill()
             fill()
 
-        nc.scalar.dma_start(out=w_bf[:], in_=ln2_w.partition_broadcast(P))
-        nc.scalar.dma_start(out=b_bf[:], in_=ln2_b.partition_broadcast(P))
         load(0)
         load(1)
         load(2)
-        nc.vector.tensor_copy(out=w_f[:], in_=w_bf[:])
-        nc.vector.tensor_copy(out=b_f[:], in_=b_bf[:])
-        top_up()
+        nc.sync.dma_start(out=w_bf[:], in_=ln2_w.partition_broadcast(P))
+        nc.sync.dma_start(out=b_bf[:], in_=ln2_b.partition_broadcast(P))
+        first = nat[0][:].bitcast(F32).rearrange("p (t q w) -> p q t w", t=PACK, w=CP)
+        for k in range(RING + XRING):
+            if k % 2 == 1:
+                banks[k] = ps_x.tile([P, PACK * P], F32, name="xb")
+            else:
+                banks[k] = ps_tr.tile([P, PACK * P], F32, name="bank")
+        for t in range(PACK):
+            for k in range(RING + XRING):
+                nc.tensor.transpose(banks[k][:, t * P:(t + 1) * P], first[:, :, t, k], ident[:])
+        st["filled"] = RING + XRING
         for k in range(WARM + AHEAD):
             leave(k % 8 in (1, 4, 6))
             top_up()
             if k % CP == AHEAD - 1 and k > CP:
                 quantise(st["quantised"])
+        nc.vector.tensor_copy(out=w_f[:], in_=w_bf[:])
+        nc.vector.tensor_copy(out=b_f[:], in_=b_bf[:])
         for b in range(XRING):
             xbank(0, b)
         for p in range(FIRST, NU):

@@ -27,11 +27,16 @@ RING = 3
 XRING = 3
 XB = NI * C // 4
 NT = NI + NU
-WARM = 3 * CP
-JG = 64
+WARM = 4 * CP
+JG = 128
 AHEAD = 3
 FIRST = -1
 SPLIT = 1
+VEX = (5,)
+TS = 3
+GSPLIT = 0
+JGE = 48
+NE = 2
 
 
 def tile_trianglemultiplication_pa_t_kernel(tc, a_proj, b_proj, ln2_w, ln2_b, out):
@@ -60,7 +65,7 @@ def tile_trianglemultiplication_pa_t_kernel(tc, a_proj, b_proj, ln2_w, ln2_b, ou
         nc.vector.memset(eps[:], EPS)
         a_codes = const.tile([P, NI, C, P], U32, name="a_codes", align_bytes=64)
         a_scales = const.tile([P, NI, C, P], U8, name="a_scales", align_bytes=64)
-        t_fixed = [const.tile([P, NI, C, P], F32, name="t0"), const.tile([P, NI, C, P], F32, name="t1")]
+        t_fixed = [const.tile([P, NI, C, P], F32, name="t%d" % i) for i in range(TS)]
 
         st = {"loaded": 0, "filled": 0, "exited": 0, "quantised": 0}
         nat = {}
@@ -170,7 +175,7 @@ def tile_trianglemultiplication_pa_t_kernel(tc, a_proj, b_proj, ln2_w, ln2_b, ou
 
         def sub(u, b):
             it, g = b // 4, b % 4
-            un[u]["t"] = t_fixed[u % 2]
+            un[u]["t"] = t_fixed[u % TS]
             nc.vector.tensor_tensor(
                 out=un[u]["t"][:, it, 4 * g:4 * g + 4, :], in0=un[u][("xb", b)],
                 in1=un[u]["mu"][:, it, :].unsqueeze(1).to_broadcast([P, 4, P]), op=ALU.subtract,
@@ -211,6 +216,15 @@ def tile_trianglemultiplication_pa_t_kernel(tc, a_proj, b_proj, ln2_w, ln2_b, ou
         def bias(u, g, engine, j0, j1):
             if "o" not in un[u]:
                 un[u]["o"] = op.tile([P, NI, P, C], F32, name="o")
+            if GSPLIT:
+                for it in range(NI):
+                    engine.tensor_tensor(
+                        out=un[u]["o"][:, it, j0:j1, 4 * g:4 * g + 4],
+                        in0=un[u]["t"][:, it, 4 * g:4 * g + 4, j0:j1].rearrange("p c j -> p j c"),
+                        in1=b_f[:, 4 * g:4 * g + 4].unsqueeze(1).to_broadcast([P, j1 - j0, 4]),
+                        op=ALU.add,
+                    )
+                return
             engine.tensor_tensor(
                 out=un[u]["o"][:, :, j0:j1, 4 * g:4 * g + 4],
                 in0=un[u]["t"][:, :, 4 * g:4 * g + 4, j0:j1].rearrange("p i c j -> p i j c"),
@@ -224,59 +238,78 @@ def tile_trianglemultiplication_pa_t_kernel(tc, a_proj, b_proj, ln2_w, ln2_b, ou
                 in_=un[u]["o"][:].rearrange("p i j c -> p i (j c)"),
             )
 
+        def scales(p, c0, c1):
+            if not 0 <= p < NU:
+                return
+            for c in range(c0, c1):
+                scale(p, c)
+                if c % 4 == 3:
+                    jg = JGE if p >= NU - NE else JG
+                    bias(p, c // 4, nc.gpsimd, 0, jg)
+                    if jg < P:
+                        bias(p, c // 4, nc.vector, jg, P)
+
         def period(p):
             nxt, nn = p + 1, p + 2
-            helper = p < 0
-            if 0 <= nxt < NU:
-                total(nxt)
-            if 0 <= p < NU:
-                for c in range(C):
-                    scale(p, c)
-                    if c % 4 == 3:
-                        bias(p, c // 4, nc.gpsimd, 0, JG)
-            leave(helper)
-            leave(False)
-            fill()
-            fill()
-            leave(helper)
-            if 0 <= nxt < NU:
-                mean(nxt)
-            fill()
-            leave(False)
-            leave(False)
-            if 0 <= nxt < NU:
-                for b in range(XB):
-                    sub(nxt, b)
-                    if b + XRING < XB:
-                        xbank(nxt, b + XRING)
-                    if b % 2 == 1:
-                        square(nxt, b // 2)
-            if 0 <= p < NU:
-                for g in range(4):
-                    bias(p, g, nc.vector, JG, P)
-                store(p)
-            if 0 <= nxt < NU:
-                chain(nxt, 0)
-            fill()
-            if 0 <= nxt < NU:
-                chain(nxt, 1)
-            fill()
-            leave(False)
-            if 0 <= nxt < NU:
-                sigma(nxt)
-            fill()
-            if st["quantised"] < NT:
-                assert st["exited"] >= min(CP * (st["quantised"] + 1), CP * NT)
+            new, old = 0 <= nxt < NU, 0 <= p < NU
+            if st["quantised"] < NT and st["exited"] >= CP * (st["quantised"] + 1):
                 quantise(st["quantised"])
-            leave(True)
+            if old:
+                chain(p, 0)
+                chain(p, 1)
             leave(False)
-            if 0 <= nxt < NU:
-                rback(nxt)
+            leave(False)
+            leave(3 in VEX)
+            fill()
+            fill()
+            fill()
+            if old:
+                sigma(p)
+                rback(p)
+            if new:
+                sub(nxt, 0)
+                sub(nxt, 1)
+                sub(nxt, 2)
+            leave(False)
+            if new:
+                square(nxt, 0)
+                xbank(nxt, 3)
+                xbank(nxt, 4)
+                xbank(nxt, 5)
+            leave(5 in VEX)
+            fill()
+            fill()
+            scales(p, 0, 2)
+            leave(False)
+            fill()
+            if new:
+                sub(nxt, 3)
+                square(nxt, 1)
+                sub(nxt, 4)
+                sub(nxt, 5)
+                xbank(nxt, 6)
+                xbank(nxt, 7)
+            if 0 <= nn < NU:
+                total(nn)
+            leave(False)
+            if new:
+                square(nxt, 2)
+            scales(p, 2, 8)
+            leave(False)
+            if 0 <= nn < NU:
+                mean(nn)
+            fill()
+            fill()
+            if new:
+                sub(nxt, 6)
+                sub(nxt, 7)
+                square(nxt, 3)
             if 0 <= nn < NU:
                 for b in range(XRING):
                     xbank(nn, b)
-            fill()
-            fill()
+            scales(p, 8, C)
+            if old:
+                store(p)
 
         load(0)
         load(1)
@@ -293,13 +326,15 @@ def tile_trianglemultiplication_pa_t_kernel(tc, a_proj, b_proj, ln2_w, ln2_b, ou
             for k in range(RING + XRING):
                 nc.tensor.transpose(banks[k][:, t * P:(t + 1) * P], first[:, :, t, k], ident[:])
         st["filled"] = RING + XRING
-        for k in range(WARM + AHEAD):
+        for k in range(WARM):
             leave(k % 8 in (1, 4, 6))
             top_up()
             if k % CP == AHEAD - 1 and k > CP:
                 quantise(st["quantised"])
         nc.vector.tensor_copy(out=w_f[:], in_=w_bf[:])
         nc.vector.tensor_copy(out=b_f[:], in_=b_bf[:])
+        total(0)
+        mean(0)
         for b in range(XRING):
             xbank(0, b)
         for p in range(FIRST, NU):

@@ -33,6 +33,13 @@ AHEAD = 3
 FIRST = -1
 SPLIT = 1
 VEX = (5,)
+HEAD = "SVGSVGSV"
+EARLY = {-1: "GSVGVSGV", 0: "SSSSVSSS"}
+STEADY = "SSSSVSSS"
+WB = 4
+NS = 3
+LATE = 3
+HL = 10
 TS = 3
 GSPLIT = 0
 JGE = 48
@@ -49,6 +56,7 @@ def tile_trianglemultiplication_pa_t_kernel(tc, a_proj, b_proj, ln2_w, ln2_b, ou
         sqp = ctx.enter_context(tc.tile_pool(name="sqp", bufs=1))
         op = ctx.enter_context(tc.tile_pool(name="op", bufs=2))
         small = ctx.enter_context(tc.tile_pool(name="small", bufs=2))
+        wordp = ctx.enter_context(tc.tile_pool(name="wordp", bufs=WB))
         ps_tr = ctx.enter_context(tc.psum_pool(name="ps_tr", bufs=RING))
         ps_x = ctx.enter_context(tc.psum_pool(name="ps_x", bufs=XRING))
         ps_stat = ctx.enter_context(tc.psum_pool(name="ps_stat", bufs=1))
@@ -109,7 +117,7 @@ def tile_trianglemultiplication_pa_t_kernel(tc, a_proj, b_proj, ln2_w, ln2_b, ou
             while st["filled"] < min(st["exited"] + ring, CP * NT):
                 fill()
 
-        def leave(on_vector):
+        def leave(route):
             k = st["exited"]
             if k >= CP * NT:
                 return
@@ -119,10 +127,17 @@ def tile_trianglemultiplication_pa_t_kernel(tc, a_proj, b_proj, ln2_w, ln2_b, ou
                 grouped[n] = grp.tile([P, C, P, PACK], BF16, name="grouped", align_bytes=64)
             src = banks[k][:].bitcast(BF16).rearrange("p (t r e) -> p e r t", t=PACK, e=2)
             dst = grouped[n][:, 2 * w:2 * w + 2, :, :]
-            if on_vector:
+            if route == "V":
                 nc.vector.tensor_copy(out=dst, in_=src)
-            else:
+            elif route == "S":
                 nc.scalar.copy(out=dst, in_=src)
+            else:
+                wb = wordp.tile([P, P * PACK], F32, name="wb")
+                nc.scalar.copy(out=wb[:].rearrange("p (r t) -> p r t", t=PACK),
+                               in_=banks[k][:].rearrange("p (t r) -> p r t", t=PACK))
+                nc.gpsimd.tensor_scalar(
+                    out=dst, in0=wb[:].bitcast(BF16).rearrange("p (r t e) -> p e r t", t=PACK, e=2),
+                    scalar1=1.0, scalar2=0.0, op0=ALU.mult, op1=ALU.add)
             st["exited"] = k + 1
 
         def quantise(n):
@@ -188,8 +203,10 @@ def tile_trianglemultiplication_pa_t_kernel(tc, a_proj, b_proj, ln2_w, ln2_b, ou
             nc.scalar.activation(out=un[u]["sq"][:, it, cs, :], in_=un[u]["t"][:, it, cs, :], func=ACT.Square)
 
         def chain(u, it):
-            if it == 0:
-                un[u]["q_t"] = ps_stat.tile([P, NI, P], F32, name="stat")
+            if it == 0 and u > NU - LATE:
+                un[u]["q_t"] = ps_tr.tile([P, PACK * P], F32, name="bank")[:, 0:NI * P].rearrange("p (i j) -> p i j", i=NI)
+            elif it == 0:
+                un[u]["q_t"] = ps_stat.tile([P, NI, P], F32, name="stat")[:]
             for c in range(C):
                 nc.tensor.matmul(
                     out=un[u]["q_t"][:, it, :], lhsT=un[u]["sq"][:, it, c, :], rhs=ident[:],
@@ -199,17 +216,20 @@ def tile_trianglemultiplication_pa_t_kernel(tc, a_proj, b_proj, ln2_w, ln2_b, ou
         def sigma(u):
             un[u]["r_t"] = small.tile([P, NI, P], F32, name="r_t")
             nc.scalar.activation(
-                out=un[u]["r_t"][:], in_=un[u]["q_t"][:], func=ACT.Abs_reciprocal_sqrt, scale=1.0 / C, bias=eps[:])
+                out=un[u]["r_t"][:], in_=un[u]["q_t"], func=ACT.Abs_reciprocal_sqrt, scale=1.0 / C, bias=eps[:])
 
         def rback(u):
-            un[u]["r"] = ps_r.tile([P, NI, P], F32, name="r")
+            if u > NU - LATE:
+                un[u]["r"] = ps_tr.tile([P, PACK * P], F32, name="bank")[:, 0:NI * P].rearrange("p (i j) -> p i j", i=NI)
+            else:
+                un[u]["r"] = ps_r.tile([P, NI, P], F32, name="r")[:]
             for it in range(NI):
                 nc.tensor.transpose(un[u]["r"][:, it, :], un[u]["r_t"][:, it, :], ident[:])
 
         def scale(u, c):
             t = un[u]["t"]
             nc.vector.scalar_tensor_tensor(
-                out=t[:, :, c, :], in0=t[:, :, c, :], scalar=w_f[:, c:c + 1], in1=un[u]["r"][:],
+                out=t[:, :, c, :], in0=t[:, :, c, :], scalar=w_f[:, c:c + 1], in1=un[u]["r"],
                 op0=ALU.mult, op1=ALU.mult,
             )
 
@@ -243,7 +263,18 @@ def tile_trianglemultiplication_pa_t_kernel(tc, a_proj, b_proj, ln2_w, ln2_b, ou
                 return
             for c in range(c0, c1):
                 scale(p, c)
-                if c % 4 == 3:
+                if p >= NU - NS:
+                    t = un[p]["t"]
+                    nc.scalar.activation(out=t[:, :, c, :], in_=t[:, :, c, :], func=ACT.Identity, bias=b_f[:, c:c + 1])
+                    if c % 4 == 3:
+                        g = c // 4
+                        if "o" not in un[p]:
+                            un[p]["o"] = op.tile([P, NI, P, C], F32, name="o")
+                        nc.gpsimd.tensor_scalar(
+                            out=un[p]["o"][:, :, :, 4 * g:4 * g + 4],
+                            in0=t[:, :, 4 * g:4 * g + 4, :].rearrange("p i c j -> p i j c"),
+                            scalar1=1.0, scalar2=0.0, op0=ALU.mult, op1=ALU.add)
+                elif c % 4 == 3:
                     jg = JGE if p >= NU - NE else JG
                     bias(p, c // 4, nc.gpsimd, 0, jg)
                     if jg < P:
@@ -251,15 +282,16 @@ def tile_trianglemultiplication_pa_t_kernel(tc, a_proj, b_proj, ln2_w, ln2_b, ou
 
         def period(p):
             nxt, nn = p + 1, p + 2
+            rt = EARLY.get(p, STEADY)
             new, old = 0 <= nxt < NU, 0 <= p < NU
             if st["quantised"] < NT and st["exited"] >= CP * (st["quantised"] + 1):
                 quantise(st["quantised"])
             if old:
                 chain(p, 0)
                 chain(p, 1)
-            leave(False)
-            leave(False)
-            leave(3 in VEX)
+            leave(rt[0])
+            leave(rt[1])
+            leave(rt[2])
             fill()
             fill()
             fill()
@@ -270,17 +302,17 @@ def tile_trianglemultiplication_pa_t_kernel(tc, a_proj, b_proj, ln2_w, ln2_b, ou
                 sub(nxt, 0)
                 sub(nxt, 1)
                 sub(nxt, 2)
-            leave(False)
+            leave(rt[3])
             if new:
                 square(nxt, 0)
                 xbank(nxt, 3)
                 xbank(nxt, 4)
                 xbank(nxt, 5)
-            leave(5 in VEX)
+            leave(rt[4])
             fill()
             fill()
             scales(p, 0, 2)
-            leave(False)
+            leave(rt[5])
             fill()
             if new:
                 sub(nxt, 3)
@@ -291,11 +323,11 @@ def tile_trianglemultiplication_pa_t_kernel(tc, a_proj, b_proj, ln2_w, ln2_b, ou
                 xbank(nxt, 7)
             if 0 <= nn < NU:
                 total(nn)
-            leave(False)
+            leave(rt[6])
             if new:
                 square(nxt, 2)
             scales(p, 2, 8)
-            leave(False)
+            leave(rt[7])
             if 0 <= nn < NU:
                 mean(nn)
             fill()
@@ -310,6 +342,37 @@ def tile_trianglemultiplication_pa_t_kernel(tc, a_proj, b_proj, ln2_w, ln2_b, ou
             scales(p, 8, C)
             if old:
                 store(p)
+
+        def stats(u):
+            chain(u, 0)
+            chain(u, 1)
+            sigma(u)
+            rback(u)
+
+        def late(p):
+            nxt, nn = p + 1, p + 2
+            new = nxt < NU
+            if st["quantised"] < NT:
+                quantise(st["quantised"])
+            if "r" not in un[p]:
+                stats(p)
+            if new:
+                for b in range(XB):
+                    sub(nxt, b)
+                    if b % 2 == 1:
+                        square(nxt, b // 2)
+                    if b + XRING < XB:
+                        xbank(nxt, b + XRING)
+                if nn < NU:
+                    total(nn)
+                    mean(nn)
+                    for b in range(XRING):
+                        xbank(nn, b)
+            scales(p, 0, HL)
+            if new:
+                stats(nxt)
+            scales(p, HL, C)
+            store(p)
 
         load(0)
         load(1)
@@ -327,7 +390,7 @@ def tile_trianglemultiplication_pa_t_kernel(tc, a_proj, b_proj, ln2_w, ln2_b, ou
                 nc.tensor.transpose(banks[k][:, t * P:(t + 1) * P], first[:, :, t, k], ident[:])
         st["filled"] = RING + XRING
         for k in range(WARM):
-            leave(k % 8 in (1, 4, 6))
+            leave(HEAD[k % len(HEAD)])
             top_up()
             if k % CP == AHEAD - 1 and k > CP:
                 quantise(st["quantised"])
@@ -338,4 +401,7 @@ def tile_trianglemultiplication_pa_t_kernel(tc, a_proj, b_proj, ln2_w, ln2_b, ou
         for b in range(XRING):
             xbank(0, b)
         for p in range(FIRST, NU):
-            period(p)
+            if p >= NU - LATE:
+                late(p)
+            else:
+                period(p)

@@ -61,7 +61,6 @@ def tile_trianglemultiplication_pa_t_kernel(tc, a_proj, b_proj, ln2_w, ln2_b, ou
         ps_x = ctx.enter_context(tc.psum_pool(name="ps_x", bufs=XRING))
         ps_stat = ctx.enter_context(tc.psum_pool(name="ps_stat", bufs=1))
         ps_r = ctx.enter_context(tc.psum_pool(name="ps_r", bufs=1))
-        ctx.enter_context(tc.manual_schedule())
 
         ident = const.tile([P, P], F32, name="ident")
         make_identity(nc, ident[:])

from contextlib import ExitStack

import concourse.mybir as mybir
from concourse.masks import make_identity

F32 = mybir.dt.float32
BF16 = mybir.dt.bfloat16
U32 = mybir.dt.uint32
U8 = mybir.dt.uint8
FP8X4 = mybir.dt.float8_e4m3fn_x4
ALU = mybir.AluOpType
ACT = mybir.ActivationFunctionType

P = 128
K = 512
C = 16
BI = 256
BJ = 1024
PACK = 4
CP = C // 2
NI = BI // P
NU = BJ // P
EPS = 1e-5
FLOPS = 2 * C * BI * BJ * K

RING = 3
XRING = 3
XB = NI * C // 4
NT = NI + NU
WARM = 4 * CP
JG = 128
AHEAD = 3
FIRST = -1
SPLIT = 1
VEX = (5,)
HEAD = "SVGSVGSV"
EARLY = {-1: "GSVGVSGV", 0: "SSSSVSSS"}
STEADY = "SSSSVSSS"
WB = 4
NS = 3
LATE = 3
HL = 10
TS = 3
GSPLIT = 0
JGE = 48
NE = 2


def tile_trianglemultiplication_pa_t_kernel(tc, a_proj, b_proj, ln2_w, ln2_b, out):
    nc = tc.nc
    with ExitStack() as ctx:
        const = ctx.enter_context(tc.tile_pool(name="const", bufs=1))
        natp = ctx.enter_context(tc.tile_pool(name="natp", bufs=3))
        grp = ctx.enter_context(tc.tile_pool(name="grp", bufs=2))
        bqp = ctx.enter_context(tc.tile_pool(name="bqp", bufs=2))
        sqp = ctx.enter_context(tc.tile_pool(name="sqp", bufs=1))
        op = ctx.enter_context(tc.tile_pool(name="op", bufs=2))
        small = ctx.enter_context(tc.tile_pool(name="small", bufs=2))
        wordp = ctx.enter_context(tc.tile_pool(name="wordp", bufs=WB))
        ps_tr = ctx.enter_context(tc.psum_pool(name="ps_tr", bufs=RING))
        ps_x = ctx.enter_context(tc.psum_pool(name="ps_x", bufs=XRING))
        ps_stat = ctx.enter_context(tc.psum_pool(name="ps_stat", bufs=1))
        ps_r = ctx.enter_context(tc.psum_pool(name="ps_r", bufs=1))

        ident = const.tile([P, P], F32, name="ident")
        make_identity(nc, ident[:])
        w_bf = const.tile([P, C], BF16, name="w_bf")
        b_bf = const.tile([P, C], BF16, name="b_bf")
        w_f = const.tile([P, C], F32, name="w_f")
        b_f = const.tile([P, C], F32, name="b_f")
        eps = const.tile([P, 1], F32, name="eps")
        nc.vector.memset(eps[:], EPS)
        a_codes = const.tile([P, NI, C, P], U32, name="a_codes", align_bytes=64)
        a_scales = const.tile([P, NI, C, P], U8, name="a_scales", align_bytes=64)
        t_fixed = [const.tile([P, NI, C, P], F32, name="t%d" % i) for i in range(TS)]

        st = {"loaded": 0, "filled": 0, "exited": 0, "quantised": 0}
        nat = {}
        grouped = {}
        banks = {}
        bq = {}
        un = [dict() for u in range(NU)]

        def load(n):
            src = a_proj if n < NI else b_proj
            r0 = (n if n < NI else n - NI) * P
            nat[n] = natp.tile([P, K * C], BF16, name="nat")
            pieces = PACK if n < SPLIT else 1
            kk = K // pieces
            for i in range(pieces):
                nc.sync.dma_start(
                    out=nat[n][:, i * kk * C:(i + 1) * kk * C],
                    in_=src[r0:r0 + P, i * kk:(i + 1) * kk, :].rearrange("r k c -> r (k c)"),
                )
            st["loaded"] = n + 1

        def fill():
            k = st["filled"]
            if k >= CP * NT:
                return
            assert k - st["exited"] < (RING + XRING if k < WARM else RING)
            n, w = k // CP, k % CP
            words = nat[n][:].bitcast(F32).rearrange("p (t q w) -> p q t w", t=PACK, w=CP)
            if k < WARM and k % 2 == 1:
                banks[k] = ps_x.tile([P, PACK * P], F32, name="xb")
            else:
                banks[k] = ps_tr.tile([P, PACK * P], F32, name="bank")
            for t in range(PACK):
                nc.tensor.transpose(banks[k][:, t * P:(t + 1) * P], words[:, :, t, w], ident[:])
            st["filled"] = k + 1
            if w == CP - 1 and st["loaded"] < NT:
                load(st["loaded"])

        def top_up():
            ring = RING + XRING if st["filled"] < WARM else RING
            while st["filled"] < min(st["exited"] + ring, CP * NT):
                fill()

        def leave(route):
            k = st["exited"]
            if k >= CP * NT:
                return
            assert k < st["filled"]
            n, w = k // CP, k % CP
            if w == 0:
                grouped[n] = grp.tile([P, C, P, PACK], BF16, name="grouped", align_bytes=64)
            src = banks[k][:].bitcast(BF16).rearrange("p (t r e) -> p e r t", t=PACK, e=2)
            dst = grouped[n][:, 2 * w:2 * w + 2, :, :]
            if route == "V":
                nc.vector.tensor_copy(out=dst, in_=src)
            elif route == "S":
                nc.scalar.copy(out=dst, in_=src)
            else:
                wb = wordp.tile([P, P * PACK], F32, name="wb")
                nc.scalar.copy(out=wb[:].rearrange("p (r t) -> p r t", t=PACK),
                               in_=banks[k][:].rearrange("p (t r) -> p r t", t=PACK))
                nc.gpsimd.tensor_scalar(
                    out=dst, in0=wb[:].bitcast(BF16).rearrange("p (r t e) -> p e r t", t=PACK, e=2),
                    scalar1=1.0, scalar2=0.0, op0=ALU.mult, op1=ALU.add)
            st["exited"] = k + 1

        def quantise(n):
            if n < NI:
                codes, scales = a_codes[:, n, :, :], a_scales[:, n, :, :]
            else:
                bq[n - NI] = (
                    bqp.tile([P, C, P], U32, name="b_codes", align_bytes=64),
                    bqp.tile([P, C, P], U8, name="b_scales", align_bytes=64),
                )
                codes, scales = bq[n - NI][0][:], bq[n - NI][1][:]
            for h in range(2):
                cs = slice(h * CP, (h + 1) * CP)
                nc.vector.quantize_mx(
                    out=codes[:, cs, :].rearrange("p c r -> p (c r)").bitcast(FP8X4),
                    scales=scales[:, cs, :].rearrange("p c r -> p (c r)"),
                    in_=grouped[n][:, cs, :, :].rearrange("p c r t -> p (c r t)"),
                )
            st["quantised"] = n + 1

        def prepare(n):
            assert st["exited"] >= CP * (n + 1)
            while st["quantised"] <= n:
                quantise(st["quantised"])

        def mx(dst, u, it, c, start, stop):
            nc.tensor.matmul_mx(
                out=dst,
                lhsT=a_codes[:, it, c, :].bitcast(FP8X4), lhsT_scale=a_scales[:, it, c, :],
                rhs=bq[u][0][:, c, :].bitcast(FP8X4), rhs_scale=bq[u][1][:, c, :],
                start=start, stop=stop,
            )

        def total(u):
            un[u]["acc"] = ps_stat.tile([P, NI, P], F32, name="stat")
            for it in range(NI):
                for c in range(C):
                    mx(un[u]["acc"][:, it, :], u, it, c, c == 0, c == C - 1)

        def mean(u):
            un[u]["mu"] = small.tile([P, NI, P], F32, name="mu")
            nc.scalar.activation(out=un[u]["mu"][:], in_=un[u]["acc"][:], func=ACT.Copy, scale=1.0 / C)

        def xbank(u, b):
            it, g = b // 4, b % 4
            xb = ps_x.tile([P, PACK * P], F32, name="xb").rearrange("p (c j) -> p c j", c=4)
            un[u][("xb", b)] = xb
            for e in range(4):
                mx(xb[:, e, :], u, it, 4 * g + e, True, True)

        def sub(u, b):
            it, g = b // 4, b % 4
            un[u]["t"] = t_fixed[u % TS]
            nc.vector.tensor_tensor(
                out=un[u]["t"][:, it, 4 * g:4 * g + 4, :], in0=un[u][("xb", b)],
                in1=un[u]["mu"][:, it, :].unsqueeze(1).to_broadcast([P, 4, P]), op=ALU.subtract,
            )

        def square(u, h):
            if h == 0:
                un[u]["sq"] = sqp.tile([P, NI, C, P], F32, name="sq")
            it, cs = h // 2, slice((h % 2) * CP, (h % 2 + 1) * CP)
            nc.scalar.activation(out=un[u]["sq"][:, it, cs, :], in_=un[u]["t"][:, it, cs, :], func=ACT.Square)

        def chain(u, it):
            if it == 0 and u > NU - LATE:
                un[u]["q_t"] = ps_tr.tile([P, PACK * P], F32, name="bank")[:, 0:NI * P].rearrange("p (i j) -> p i j", i=NI)
            elif it == 0:
                un[u]["q_t"] = ps_stat.tile([P, NI, P], F32, name="stat")[:]
            for c in range(C):
                nc.tensor.matmul(
                    out=un[u]["q_t"][:, it, :], lhsT=un[u]["sq"][:, it, c, :], rhs=ident[:],
                    is_transpose=True, start=(c == 0), stop=(c == C - 1),
                )

        def sigma(u):
            un[u]["r_t"] = small.tile([P, NI, P], F32, name="r_t")
            nc.scalar.activation(
                out=un[u]["r_t"][:], in_=un[u]["q_t"], func=ACT.Abs_reciprocal_sqrt, scale=1.0 / C, bias=eps[:])

        def rback(u):
            if u > NU - LATE:
                un[u]["r"] = ps_tr.tile([P, PACK * P], F32, name="bank")[:, 0:NI * P].rearrange("p (i j) -> p i j", i=NI)
            else:
                un[u]["r"] = ps_r.tile([P, NI, P], F32, name="r")[:]
            for it in range(NI):
                nc.tensor.transpose(un[u]["r"][:, it, :], un[u]["r_t"][:, it, :], ident[:])

        def scale(u, c):
            t = un[u]["t"]
            nc.vector.scalar_tensor_tensor(
                out=t[:, :, c, :], in0=t[:, :, c, :], scalar=w_f[:, c:c + 1], in1=un[u]["r"],
                op0=ALU.mult, op1=ALU.mult,
            )

        def bias(u, g, engine, j0, j1):
            if "o" not in un[u]:
                un[u]["o"] = op.tile([P, NI, P, C], F32, name="o")
            if GSPLIT:
                for it in range(NI):
                    engine.tensor_tensor(
                        out=un[u]["o"][:, it, j0:j1, 4 * g:4 * g + 4],
                        in0=un[u]["t"][:, it, 4 * g:4 * g + 4, j0:j1].rearrange("p c j -> p j c"),
                        in1=b_f[:, 4 * g:4 * g + 4].unsqueeze(1).to_broadcast([P, j1 - j0, 4]),
                        op=ALU.add,
                    )
                return
            engine.tensor_tensor(
                out=un[u]["o"][:, :, j0:j1, 4 * g:4 * g + 4],
                in0=un[u]["t"][:, :, 4 * g:4 * g + 4, j0:j1].rearrange("p i c j -> p i j c"),
                in1=b_f[:, 4 * g:4 * g + 4].unsqueeze(1).unsqueeze(1).to_broadcast([P, NI, j1 - j0, 4]),
                op=ALU.add,
            )

        def store(u):
            nc.sync.dma_start(
                out=out[:, u * P:(u + 1) * P, :].rearrange("(i p) j c -> p i (j c)", p=P),
                in_=un[u]["o"][:].rearrange("p i j c -> p i (j c)"),
            )

        def scales(p, c0, c1):
            if not 0 <= p < NU:
                return
            for c in range(c0, c1):
                scale(p, c)
                if p >= NU - NS:
                    t = un[p]["t"]
                    nc.scalar.activation(out=t[:, :, c, :], in_=t[:, :, c, :], func=ACT.Identity, bias=b_f[:, c:c + 1])
                    if c % 4 == 3:
                        g = c // 4
                        if "o" not in un[p]:
                            un[p]["o"] = op.tile([P, NI, P, C], F32, name="o")
                        nc.gpsimd.tensor_scalar(
                            out=un[p]["o"][:, :, :, 4 * g:4 * g + 4],
                            in0=t[:, :, 4 * g:4 * g + 4, :].rearrange("p i c j -> p i j c"),
                            scalar1=1.0, scalar2=0.0, op0=ALU.mult, op1=ALU.add)
                elif c % 4 == 3:
                    jg = JGE if p >= NU - NE else JG
                    bias(p, c // 4, nc.gpsimd, 0, jg)
                    if jg < P:
                        bias(p, c // 4, nc.vector, jg, P)

        def period(p):
            nxt, nn = p + 1, p + 2
            rt = EARLY.get(p, STEADY)
            new, old = 0 <= nxt < NU, 0 <= p < NU
            if st["quantised"] < NT and st["exited"] >= CP * (st["quantised"] + 1):
                quantise(st["quantised"])
            if old:
                chain(p, 0)
                chain(p, 1)
            leave(rt[0])
            leave(rt[1])
            leave(rt[2])
            fill()
            fill()
            fill()
            if old:
                sigma(p)
                rback(p)
            if new:
                sub(nxt, 0)
                sub(nxt, 1)
                sub(nxt, 2)
            leave(rt[3])
            if new:
                square(nxt, 0)
                xbank(nxt, 3)
                xbank(nxt, 4)
                xbank(nxt, 5)
            leave(rt[4])
            fill()
            fill()
            scales(p, 0, 2)
            leave(rt[5])
            fill()
            if new:
                sub(nxt, 3)
                square(nxt, 1)
                sub(nxt, 4)
                sub(nxt, 5)
                xbank(nxt, 6)
                xbank(nxt, 7)
            if 0 <= nn < NU:
                total(nn)
            leave(rt[6])
            if new:
                square(nxt, 2)
            scales(p, 2, 8)
            leave(rt[7])
            if 0 <= nn < NU:
                mean(nn)
            fill()
            fill()
            if new:
                sub(nxt, 6)
                sub(nxt, 7)
                square(nxt, 3)
            if 0 <= nn < NU:
                for b in range(XRING):
                    xbank(nn, b)
            scales(p, 8, C)
            if old:
                store(p)

        def stats(u):
            chain(u, 0)
            chain(u, 1)
            sigma(u)
            rback(u)

        def late(p):
            nxt, nn = p + 1, p + 2
            new = nxt < NU
            if st["quantised"] < NT:
                quantise(st["quantised"])
            if "r" not in un[p]:
                stats(p)
            if new:
                for b in range(XB):
                    sub(nxt, b)
                    if b % 2 == 1:
                        square(nxt, b // 2)
                    if b + XRING < XB:
                        xbank(nxt, b + XRING)
                if nn < NU:
                    total(nn)
                    mean(nn)
                    for b in range(XRING):
                        xbank(nn, b)
            scales(p, 0, HL)
            if new:
                stats(nxt)
            scales(p, HL, C)
            store(p)

        load(0)
        load(1)
        load(2)
        nc.sync.dma_start(out=w_bf[:], in_=ln2_w.partition_broadcast(P))
        nc.sync.dma_start(out=b_bf[:], in_=ln2_b.partition_broadcast(P))
        first = nat[0][:].bitcast(F32).rearrange("p (t q w) -> p q t w", t=PACK, w=CP)
        for k in range(RING + XRING):
            if k % 2 == 1:
                banks[k] = ps_x.tile([P, PACK * P], F32, name="xb")
            else:
                banks[k] = ps_tr.tile([P, PACK * P], F32, name="bank")
        for t in range(PACK):
            for k in range(RING + XRING):
                nc.tensor.transpose(banks[k][:, t * P:(t + 1) * P], first[:, :, t, k], ident[:])
        st["filled"] = RING + XRING
        for k in range(WARM):
            leave(HEAD[k % len(HEAD)])
            top_up()
            if k % CP == AHEAD - 1 and k > CP:
                quantise(st["quantised"])
        nc.vector.tensor_copy(out=w_f[:], in_=w_bf[:])
        nc.vector.tensor_copy(out=b_f[:], in_=b_bf[:])
        total(0)
        mean(0)
        for b in range(XRING):
            xbank(0, b)
        for p in range(FIRST, NU):
            if p >= NU - LATE:
                late(p)
            else:
                period(p)
